import numpy as np
import ml_dtypes

BF16 = ml_dtypes.bfloat16


def bf(x):
    return np.asarray(x, np.float32).astype(BF16)


def f32(x):
    return np.asarray(x, np.float32)


def f64(x):
    return np.asarray(x).astype(np.float64)


def striped(idx):
    return np.tile(idx.reshape(-1, 16).T, (8, 1))


C, V, T, K, N = 512, 256, 256, 4, 1024
EPS = 1e-5


def pos_code():
    i = np.arange(C)
    e = np.where(i % 2 == 0, i, i - 1).astype(np.float32) / np.float32(C)
    const = np.power(np.float32(10000.0), e).astype(np.float32)
    ang = np.arange(T, dtype=np.float32)[None, :] / const[:, None]
    return np.where((i % 2 == 0)[:, None], np.sin(ang), np.cos(ang))


def setup_inputs():
    return {"emb": f32(np.random.standard_normal((C, V))), "pos": f32(pos_code()), "offs": striped(np.concatenate([np.random.permutation(V) for _ in range(K)]))}


def reference(emb, pos, offs):
    idx = offs[:16].T.reshape(-1)
    h = f64(emb)[:, idx] + np.tile(f64(pos), (1, K))
    m = h.mean(axis=0, keepdims=True)
    v = ((h - m) ** 2).mean(axis=0, keepdims=True)
    return (h - m) / np.sqrt(v + EPS)

@@ -1,0 +1,77 @@
+import concourse.mybir as mybir
+
+F32, BF16, U16 = mybir.dt.float32, mybir.dt.bfloat16, mybir.dt.uint16
+ALU = mybir.AluOpType
+FUNC = mybir.ActivationFunctionType
+
+P = 128
+C, V, T, K = 512, 256, 256, 4
+N = K * T
+CB = C // P
+EPS = 1e-5
+FLOPS = 2 * 2 * C * N
+
+
+def tile_first_decoder_kernel(tc, emb, pos, offs, out):
+    nc = tc.nc
+    emb_blocks = emb.rearrange("(b p) v -> b p v", p=P)
+    pos_blocks = pos.rearrange("(b p) t -> b p t", p=P)
+    out_blocks = out.rearrange("(b p) j -> p b j", p=P)
+
+    with (
+        tc.tile_pool(name="held", bufs=1) as held,
+        tc.tile_pool(name="work", bufs=K) as work,
+        tc.psum_pool(name="psum", bufs=K) as psum,
+    ):
+        offsets = held.tile([P, N // 16], U16, name="offsets")
+        nc.sync.dma_start(offsets[:], offs)
+        tables, codes = [], []
+        for b in range(CB):
+            table = held.tile([P, V], F32, name=f"table{b}")
+            nc.sync.dma_start(table[:], emb_blocks[b])
+            tables.append(table)
+            code = held.tile([P, T], F32, name=f"code{b}")
+            nc.scalar.dma_start(code[:], pos_blocks[b])
+            codes.append(code)
+
+        average = held.tile([P, P], BF16, name="average")
+        nc.vector.memset(average[:], 1.0 / C)
+        eps = held.tile([P, 1], F32, name="eps")
+        nc.vector.memset(eps[:], EPS)
+
+        hs, means = [], []
+        for k in range(K):
+            piece = offsets[:, k * (T // 16) : (k + 1) * (T // 16)]
+            h = work.tile([P, CB, T], F32, name="h")
+            for b in range(CB):
+                nc.vector.tensor_tensor(h[:, b, :], tables[b][:].indirect(piece), codes[b][:], ALU.add)
+            h16 = work.tile([P, CB, T], BF16, name="h16")
+            nc.scalar.copy(h16[:], h[:])
+            mean = psum.tile([P, T], F32, name="mean")
+            for b in range(CB):
+                nc.tensor.matmul(mean[:], average[:], h16[:, b, :], start=(b == 0), stop=(b == CB - 1))
+            hs.append(h)
+            means.append(mean)
+
+        centred, rstds = [], []
+        for k in range(K):
+            d = work.tile([P, CB, T], F32, name="d")
+            nc.vector.tensor_tensor(
+                d[:], hs[k][:], means[k][:].unsqueeze(1).to_broadcast([P, CB, T]), ALU.subtract
+            )
+            squares = work.tile([P, CB, T], BF16, name="squares")
+            nc.scalar.activation(squares[:], d[:], FUNC.Square)
+            var = psum.tile([P, T], F32, name="var")
+            for b in range(CB):
+                nc.tensor.matmul(var[:], average[:], squares[:, b, :], start=(b == 0), stop=(b == CB - 1))
+            rstd = work.tile([P, T], F32, name="rstd")
+            nc.scalar.activation(rstd[:], var[:], FUNC.Abs_reciprocal_sqrt, bias=eps[:])
+            centred.append(d)
+            rstds.append(rstd)
+
+        for k in range(K):
+            y = work.tile([P, CB, T], F32, name="y")
+            nc.vector.tensor_tensor(
+                y[:], centred[k][:], rstds[k][:].unsqueeze(1).to_broadcast([P, CB, T]), ALU.mult
+            )
+            nc.sync.dma_start(out_blocks[:, :, k * T : (k + 1) * T], y[:])

@@ -39,6 +39,9 @@ def tile_first_decoder_kernel(tc, emb, pos, offs, out):
         eps = held.tile([P, 1], F32, name="eps")
         nc.vector.memset(eps[:], EPS)
 
+        warm = held.tile([P, 1], F32, name="warm")
+        nc.scalar.activation(warm[:], eps[:], FUNC.Abs_reciprocal_sqrt)
+
         hs, means = [], []
         for k in range(K):
             piece = offsets[:, k * (T // 16) : (k + 1) * (T // 16)]

@@ -9,6 +9,7 @@ C, V, T, K = 512, 256, 256, 4
 N = K * T
 CB = C // P
 EPS = 1e-5
+PAIR = 2
 FLOPS = 2 * 2 * C * N
 
 
@@ -49,10 +50,11 @@ def tile_first_decoder_kernel(tc, emb, pos, offs, out):
             for b in range(CB):
                 nc.vector.tensor_tensor(h[:, b, :], tables[b][:].indirect(piece), codes[b][:], ALU.add)
             h16 = work.tile([P, CB, T], BF16, name="h16")
-            nc.scalar.copy(h16[:], h[:])
             mean = psum.tile([P, T], F32, name="mean")
-            for b in range(CB):
-                nc.tensor.matmul(mean[:], average[:], h16[:, b, :], start=(b == 0), stop=(b == CB - 1))
+            for pair in range(0, CB, PAIR):
+                nc.scalar.copy(h16[:, pair : pair + PAIR, :], h[:, pair : pair + PAIR, :])
+                for b in range(pair, pair + PAIR):
+                    nc.tensor.matmul(mean[:], average[:], h16[:, b, :], start=(b == 0), stop=(b == CB - 1))
             hs.append(h)
             means.append(mean)
 
@@ -63,10 +65,11 @@ def tile_first_decoder_kernel(tc, emb, pos, offs, out):
                 d[:], hs[k][:], means[k][:].unsqueeze(1).to_broadcast([P, CB, T]), ALU.subtract
             )
             squares = work.tile([P, CB, T], BF16, name="squares")
-            nc.scalar.activation(squares[:], d[:], FUNC.Square)
             var = psum.tile([P, T], F32, name="var")
-            for b in range(CB):
-                nc.tensor.matmul(var[:], average[:], squares[:, b, :], start=(b == 0), stop=(b == CB - 1))
+            for pair in range(0, CB, PAIR):
+                nc.scalar.activation(squares[:, pair : pair + PAIR, :], d[:, pair : pair + PAIR, :], FUNC.Square)
+                for b in range(pair, pair + PAIR):
+                    nc.tensor.matmul(var[:], average[:], squares[:, b, :], start=(b == 0), stop=(b == CB - 1))
             rstd = work.tile([P, T], F32, name="rstd")
             nc.scalar.activation(rstd[:], var[:], FUNC.Abs_reciprocal_sqrt, bias=eps[:])
             centred.append(d)

@@ -50,11 +50,10 @@ def tile_first_decoder_kernel(tc, emb, pos, offs, out):
             for b in range(CB):
                 nc.vector.tensor_tensor(h[:, b, :], tables[b][:].indirect(piece), codes[b][:], ALU.add)
             h16 = work.tile([P, CB, T], BF16, name="h16")
+            nc.scalar.copy(h16[:], h[:])
             mean = psum.tile([P, T], F32, name="mean")
-            for pair in range(0, CB, PAIR):
-                nc.scalar.copy(h16[:, pair : pair + PAIR, :], h[:, pair : pair + PAIR, :])
-                for b in range(pair, pair + PAIR):
-                    nc.tensor.matmul(mean[:], average[:], h16[:, b, :], start=(b == 0), stop=(b == CB - 1))
+            for b in range(CB):
+                nc.tensor.matmul(mean[:], average[:], h16[:, b, :], start=(b == 0), stop=(b == CB - 1))
             hs.append(h)
             means.append(mean)
 
@@ -65,19 +64,22 @@ def tile_first_decoder_kernel(tc, emb, pos, offs, out):
                 d[:], hs[k][:], means[k][:].unsqueeze(1).to_broadcast([P, CB, T]), ALU.subtract
             )
             squares = work.tile([P, CB, T], BF16, name="squares")
+            nc.scalar.activation(squares[:], d[:], FUNC.Square)
             var = psum.tile([P, T], F32, name="var")
-            for pair in range(0, CB, PAIR):
-                nc.scalar.activation(squares[:, pair : pair + PAIR, :], d[:, pair : pair + PAIR, :], FUNC.Square)
-                for b in range(pair, pair + PAIR):
-                    nc.tensor.matmul(var[:], average[:], squares[:, b, :], start=(b == 0), stop=(b == CB - 1))
+            for b in range(CB):
+                nc.tensor.matmul(var[:], average[:], squares[:, b, :], start=(b == 0), stop=(b == CB - 1))
             rstd = work.tile([P, T], F32, name="rstd")
             nc.scalar.activation(rstd[:], var[:], FUNC.Abs_reciprocal_sqrt, bias=eps[:])
             centred.append(d)
             rstds.append(rstd)
 
         for k in range(K):
-            y = work.tile([P, CB, T], F32, name="y")
-            nc.vector.tensor_tensor(
-                y[:], centred[k][:], rstds[k][:].unsqueeze(1).to_broadcast([P, CB, T]), ALU.mult
-            )
-            nc.sync.dma_start(out_blocks[:, :, k * T : (k + 1) * T], y[:])
+            for pair in range(0, CB, PAIR):
+                y = work.tile([P, PAIR, T], F32, name=f"y{pair}")
+                nc.vector.tensor_tensor(
+                    y[:],
+                    centred[k][:, pair : pair + PAIR, :],
+                    rstds[k][:].unsqueeze(1).to_broadcast([P, PAIR, T]),
+                    ALU.mult,
+                )
+                nc.sync.dma_start(out_blocks[:, pair : pair + PAIR, k * T : (k + 1) * T], y[:])

@@ -25,11 +25,12 @@ def tile_first_decoder_kernel(tc, emb, pos, offs, out):
         tc.psum_pool(name="psum", bufs=K) as psum,
     ):
         offsets = held.tile([P, N // 16], U16, name="offsets")
-        nc.sync.dma_start(offsets[:], offs)
         tables, codes = [], []
         for b in range(CB):
             table = held.tile([P, V], F32, name=f"table{b}")
             nc.sync.dma_start(table[:], emb_blocks[b])
+            if b == 0:
+                nc.sync.dma_start(offsets[:], offs)
             tables.append(table)
             code = held.tile([P, T], F32, name=f"code{b}")
             nc.scalar.dma_start(code[:], pos_blocks[b])
@@ -74,12 +75,13 @@ def tile_first_decoder_kernel(tc, emb, pos, offs, out):
             rstds.append(rstd)
 
         for k in range(K):
-            for pair in range(0, CB, PAIR):
-                y = work.tile([P, PAIR, T], F32, name=f"y{pair}")
+            step = PAIR if k < K - 1 else 1
+            for first in range(0, CB, step):
+                y = work.tile([P, step, T], F32, name=f"y{first}_{step}")
                 nc.vector.tensor_tensor(
                     y[:],
-                    centred[k][:, pair : pair + PAIR, :],
-                    rstds[k][:].unsqueeze(1).to_broadcast([P, PAIR, T]),
+                    centred[k][:, first : first + step, :],
+                    rstds[k][:].unsqueeze(1).to_broadcast([P, step, T]),
                     ALU.mult,
                 )
-                nc.sync.dma_start(out_blocks[:, pair : pair + PAIR, k * T : (k + 1) * T], y[:])
+                nc.sync.dma_start(out_blocks[:, first : first + step, k * T : (k + 1) * T], y[:])

@@ -5,12 +5,28 @@ ALU = mybir.AluOpType
 FUNC = mybir.ActivationFunctionType
 
 P = 128
+QUADRANT = 32
 C, V, T, K = 512, 256, 256, 4
 N = K * T
 CB = C // P
+TB = T // P
+FLIPPED = 2
 EPS = 1e-5
 PAIR = 2
 FLOPS = 2 * 2 * C * N
+
+
+def write_identity(nc, pool, identity):
+    ones = pool.tile([P, QUADRANT], F32, name="ones")
+    nc.vector.memset(ones[:], 1.0)
+    counts = pool.tile([P, QUADRANT], F32, name="counts", align_bytes=64)
+    nc.vector.tensor_tensor_scan(counts[:], ones[:], ones[:], 0.0, ALU.mult, ALU.add)
+    counts_turned = pool.tile([P, QUADRANT], F32, name="counts_turned", align_bytes=64)
+    nc.vector.transpose(counts_turned[:], counts[:])
+    nc.vector.memset(identity[:], 0.0)
+    for q in range(0, P, QUADRANT):
+        rows = slice(q, q + QUADRANT)
+        nc.vector.tensor_tensor(identity[rows, rows], counts[rows, :], counts_turned[rows, :], ALU.is_equal)
 
 
 def tile_first_decoder_kernel(tc, emb, pos, offs, out):
@@ -21,8 +37,12 @@ def tile_first_decoder_kernel(tc, emb, pos, offs, out):
 
     with (
         tc.tile_pool(name="held", bufs=1) as held,
-        tc.tile_pool(name="work", bufs=K) as work,
-        tc.psum_pool(name="psum", bufs=K) as psum,
+        tc.tile_pool(name="looked_up", bufs=1) as looked_up,
+        tc.tile_pool(name="flip", bufs=FLIPPED * TB) as flip,
+        tc.tile_pool(name="work", bufs=K - FLIPPED) as work,
+        tc.psum_pool(name="flips", bufs=4) as flips,
+        tc.psum_pool(name="backs", bufs=2) as backs,
+        tc.psum_pool(name="sums", bufs=2) as sums,
     ):
         offsets = held.tile([P, N // 16], U16, name="offsets")
         tables, codes = [], []
@@ -35,46 +55,86 @@ def tile_first_decoder_kernel(tc, emb, pos, offs, out):
             code = held.tile([P, T], F32, name=f"code{b}")
             nc.scalar.dma_start(code[:], pos_blocks[b])
             codes.append(code)
+        later_codes = held.tile([P, CB, T], F32, name="later_codes")
+        nc.scalar.dma_start(later_codes[:], pos.rearrange("(b p) t -> p b t", p=P))
 
-        average = held.tile([P, P], BF16, name="average")
-        nc.vector.memset(average[:], 1.0 / C)
         eps = held.tile([P, 1], F32, name="eps")
         nc.vector.memset(eps[:], EPS)
-
         warm = held.tile([P, 1], F32, name="warm")
         nc.scalar.activation(warm[:], eps[:], FUNC.Abs_reciprocal_sqrt)
 
-        hs, means = [], []
-        for k in range(K):
+        average = held.tile([P, P], F32, name="average")
+        nc.vector.memset(average[:], 1.0 / C)
+        average16 = held.tile([P, P], BF16, name="average16")
+        nc.vector.memset(average16[:], 1.0 / C)
+        identity = held.tile([P, P], F32, name="identity")
+        write_identity(nc, held, identity)
+
+        for k in range(FLIPPED):
+            piece = offsets[:, k * (T // 16) : (k + 1) * (T // 16)]
+            flipped = [flips.tile([P, C], F32, name="flipped") for t in range(TB)]
+            for b in range(CB):
+                h = looked_up.tile([P, T], F32, name=f"h{b}")
+                code = codes[b][:] if k == 0 else later_codes[:, b, :]
+                nc.vector.tensor_tensor(h[:], tables[b][:].indirect(piece), code, ALU.add)
+                for t in range(TB):
+                    nc.tensor.transpose(flipped[t][:, b * P : (b + 1) * P], h[:, t * P : (t + 1) * P], identity[:])
+            minus_means = []
+            for t in range(TB):
+                unread = flip.tile([P, C], F32, name="unread")
+                minus_mean = flip.tile([P, 1], F32, name="minus_mean")
+                nc.scalar.activation(unread[:], flipped[t][:], FUNC.Copy, scale=-1.0 / C, accum_out=minus_mean[:])
+                minus_means.append(minus_mean)
+            scales, shifts = [], []
+            for t in range(TB):
+                unread = flip.tile([P, C], F32, name="unread")
+                squared = flip.tile([P, 1], F32, name="squared")
+                nc.scalar.activation(
+                    unread[:], flipped[t][:], FUNC.Square, bias=minus_means[t][:], accum_out=squared[:]
+                )
+                scale = flip.tile([P, 1], F32, name="scale")
+                nc.scalar.activation(scale[:], squared[:], FUNC.Abs_reciprocal_sqrt, bias=eps[:], scale=1.0 / C)
+                shift = flip.tile([P, 1], F32, name="shift")
+                nc.scalar.activation(shift[:], minus_means[t][:], FUNC.Copy, scale=scale[:])
+                scales.append(scale)
+                shifts.append(shift)
+            for t in range(TB):
+                rows = flip.tile([P, C], F32, name="rows")
+                nc.scalar.activation(rows[:], flipped[t][:], FUNC.Identity, bias=shifts[t][:], scale=scales[t][:])
+                back = backs.tile([P, CB, P], F32, name="back")
+                for b in range(CB):
+                    nc.tensor.transpose(back[:, b, :], rows[:, b * P : (b + 1) * P], identity[:])
+                y = flip.tile([P, CB, P], F32, name="flipped_y")
+                nc.vector.tensor_copy(y[:], back[:])
+                first = k * T + t * P
+                nc.sync.dma_start(out_blocks[:, :, first : first + P], y[:])
+
+        hs, means = {}, {}
+        for k in range(FLIPPED, K):
             piece = offsets[:, k * (T // 16) : (k + 1) * (T // 16)]
             h = work.tile([P, CB, T], F32, name="h")
+            mean = sums.tile([P, T], F32, name="sum")
             for b in range(CB):
-                nc.vector.tensor_tensor(h[:, b, :], tables[b][:].indirect(piece), codes[b][:], ALU.add)
-            h16 = work.tile([P, CB, T], BF16, name="h16")
-            nc.scalar.copy(h16[:], h[:])
-            mean = psum.tile([P, T], F32, name="mean")
-            for b in range(CB):
-                nc.tensor.matmul(mean[:], average[:], h16[:, b, :], start=(b == 0), stop=(b == CB - 1))
-            hs.append(h)
-            means.append(mean)
+                nc.vector.tensor_tensor(h[:, b, :], tables[b][:].indirect(piece), later_codes[:, b, :], ALU.add)
+                nc.tensor.matmul(mean[:], average[:], h[:, b, :], start=(b == 0), stop=(b == CB - 1))
+            hs[k], means[k] = h, mean
 
-        centred, rstds = [], []
-        for k in range(K):
+        centred, rstds = {}, {}
+        for k in range(FLIPPED, K):
             d = work.tile([P, CB, T], F32, name="d")
             nc.vector.tensor_tensor(
                 d[:], hs[k][:], means[k][:].unsqueeze(1).to_broadcast([P, CB, T]), ALU.subtract
             )
             squares = work.tile([P, CB, T], BF16, name="squares")
             nc.scalar.activation(squares[:], d[:], FUNC.Square)
-            var = psum.tile([P, T], F32, name="var")
+            var = sums.tile([P, T], F32, name="sum")
             for b in range(CB):
-                nc.tensor.matmul(var[:], average[:], squares[:, b, :], start=(b == 0), stop=(b == CB - 1))
+                nc.tensor.matmul(var[:], average16[:], squares[:, b, :], start=(b == 0), stop=(b == CB - 1))
             rstd = work.tile([P, T], F32, name="rstd")
             nc.scalar.activation(rstd[:], var[:], FUNC.Abs_reciprocal_sqrt, bias=eps[:])
-            centred.append(d)
-            rstds.append(rstd)
+            centred[k], rstds[k] = d, rstd
 
-        for k in range(K):
+        for k in range(FLIPPED, K):
             step = PAIR if k < K - 1 else 1
             for first in range(0, CB, step):
                 y = work.tile([P, step, T], F32, name=f"y{first}_{step}")

@@ -10,7 +10,7 @@ C, V, T, K = 512, 256, 256, 4
 N = K * T
 CB = C // P
 TB = T // P
-FLIPPED = 2
+FLIPPED = 1
 EPS = 1e-5
 PAIR = 2
 FLOPS = 2 * 2 * C * N
@@ -40,9 +40,8 @@ def tile_first_decoder_kernel(tc, emb, pos, offs, out):
         tc.tile_pool(name="looked_up", bufs=1) as looked_up,
         tc.tile_pool(name="flip", bufs=FLIPPED * TB) as flip,
         tc.tile_pool(name="work", bufs=K - FLIPPED) as work,
-        tc.psum_pool(name="flips", bufs=4) as flips,
-        tc.psum_pool(name="backs", bufs=2) as backs,
-        tc.psum_pool(name="sums", bufs=2) as sums,
+        tc.psum_pool(name="banks", bufs=4) as banks,
+        tc.psum_pool(name="backs", bufs=TB) as backs,
     ):
         offsets = held.tile([P, N // 16], U16, name="offsets")
         tables, codes = [], []
@@ -53,10 +52,16 @@ def tile_first_decoder_kernel(tc, emb, pos, offs, out):
                 nc.sync.dma_start(offsets[:], offs)
             tables.append(table)
             code = held.tile([P, T], F32, name=f"code{b}")
-            nc.scalar.dma_start(code[:], pos_blocks[b])
+            queue = nc.scalar if b == 0 else nc.sync
+            queue.dma_start(code[:], pos_blocks[b])
             codes.append(code)
-        later_codes = held.tile([P, CB, T], F32, name="later_codes")
-        nc.scalar.dma_start(later_codes[:], pos.rearrange("(b p) t -> p b t", p=P))
+        code_copies = {}
+        for k in range(1, K):
+            copy = held.tile([P, CB, T], F32, name=f"code_copy{k}")
+            for first in range(0, CB, PAIR):
+                pair = slice(first, first + PAIR)
+                nc.sync.dma_start(copy[:, pair, :], pos.rearrange("(b p) t -> p b t", p=P)[:, pair, :])
+            code_copies[k] = copy
 
         eps = held.tile([P, 1], F32, name="eps")
         nc.vector.memset(eps[:], EPS)
@@ -72,11 +77,10 @@ def tile_first_decoder_kernel(tc, emb, pos, offs, out):
 
         for k in range(FLIPPED):
             piece = offsets[:, k * (T // 16) : (k + 1) * (T // 16)]
-            flipped = [flips.tile([P, C], F32, name="flipped") for t in range(TB)]
+            flipped = [banks.tile([P, C], F32, name="flipped", tag="bank") for t in range(TB)]
             for b in range(CB):
                 h = looked_up.tile([P, T], F32, name=f"h{b}")
-                code = codes[b][:] if k == 0 else later_codes[:, b, :]
-                nc.vector.tensor_tensor(h[:], tables[b][:].indirect(piece), code, ALU.add)
+                nc.vector.tensor_tensor(h[:], tables[b][:].indirect(piece), codes[b][:], ALU.add)
                 for t in range(TB):
                     nc.tensor.transpose(flipped[t][:, b * P : (b + 1) * P], h[:, t * P : (t + 1) * P], identity[:])
             minus_means = []
@@ -105,7 +109,7 @@ def tile_first_decoder_kernel(tc, emb, pos, offs, out):
                 for b in range(CB):
                     nc.tensor.transpose(back[:, b, :], rows[:, b * P : (b + 1) * P], identity[:])
                 y = flip.tile([P, CB, P], F32, name="flipped_y")
-                nc.vector.tensor_copy(y[:], back[:])
+                nc.scalar.copy(y[:], back[:])
                 first = k * T + t * P
                 nc.sync.dma_start(out_blocks[:, :, first : first + P], y[:])
 
@@ -113,23 +117,28 @@ def tile_first_decoder_kernel(tc, emb, pos, offs, out):
         for k in range(FLIPPED, K):
             piece = offsets[:, k * (T // 16) : (k + 1) * (T // 16)]
             h = work.tile([P, CB, T], F32, name="h")
-            mean = sums.tile([P, T], F32, name="sum")
+            mean = banks.tile([P, T], F32, name="sum", tag="bank")
             for b in range(CB):
-                nc.vector.tensor_tensor(h[:, b, :], tables[b][:].indirect(piece), later_codes[:, b, :], ALU.add)
+                nc.vector.tensor_tensor(h[:, b, :], tables[b][:].indirect(piece), code_copies[k][:, b, :], ALU.add)
                 nc.tensor.matmul(mean[:], average[:], h[:, b, :], start=(b == 0), stop=(b == CB - 1))
             hs[k], means[k] = h, mean
 
         centred, rstds = {}, {}
         for k in range(FLIPPED, K):
             d = work.tile([P, CB, T], F32, name="d")
-            nc.vector.tensor_tensor(
-                d[:], hs[k][:], means[k][:].unsqueeze(1).to_broadcast([P, CB, T]), ALU.subtract
-            )
             squares = work.tile([P, CB, T], BF16, name="squares")
-            nc.scalar.activation(squares[:], d[:], FUNC.Square)
-            var = sums.tile([P, T], F32, name="sum")
-            for b in range(CB):
-                nc.tensor.matmul(var[:], average16[:], squares[:, b, :], start=(b == 0), stop=(b == CB - 1))
+            var = banks.tile([P, T], F32, name="sum", tag="bank")
+            for first in range(0, CB, PAIR):
+                pair = slice(first, first + PAIR)
+                nc.vector.tensor_tensor(
+                    d[:, pair, :],
+                    hs[k][:, pair, :],
+                    means[k][:].unsqueeze(1).to_broadcast([P, PAIR, T]),
+                    ALU.subtract,
+                )
+                nc.scalar.activation(squares[:, pair, :], d[:, pair, :], FUNC.Square)
+                for b in range(first, first + PAIR):
+                    nc.tensor.matmul(var[:], average16[:], squares[:, b, :], start=(b == 0), stop=(b == CB - 1))
             rstd = work.tile([P, T], F32, name="rstd")
             nc.scalar.activation(rstd[:], var[:], FUNC.Abs_reciprocal_sqrt, bias=eps[:])
             centred[k], rstds[k] = d, rstd

@@ -103,7 +103,7 @@ def tile_first_decoder_kernel(tc, emb, pos, offs, out):
                 scales.append(scale)
                 shifts.append(shift)
             for t in range(TB):
-                rows = flip.tile([P, C], F32, name="rows")
+                rows = flip.tile([P, C], F32, name="rows", tag="rows")
                 nc.scalar.activation(rows[:], flipped[t][:], FUNC.Identity, bias=shifts[t][:], scale=scales[t][:])
                 back = backs.tile([P, CB, P], F32, name="back")
                 for b in range(CB):
@@ -126,7 +126,7 @@ def tile_first_decoder_kernel(tc, emb, pos, offs, out):
         centred, rstds = {}, {}
         for k in range(FLIPPED, K):
             d = work.tile([P, CB, T], F32, name="d")
-            squares = work.tile([P, CB, T], BF16, name="squares")
+            squares = flip.tile([P, CB, T], BF16, name="squares", tag="rows")
             var = banks.tile([P, T], F32, name="sum", tag="bank")
             for first in range(0, CB, PAIR):
                 pair = slice(first, first + PAIR)

import concourse.mybir as mybir

F32, BF16, U16 = mybir.dt.float32, mybir.dt.bfloat16, mybir.dt.uint16
ALU = mybir.AluOpType
FUNC = mybir.ActivationFunctionType

P = 128
QUADRANT = 32
C, V, T, K = 512, 256, 256, 4
N = K * T
CB = C // P
TB = T // P
FLIPPED = 1
EPS = 1e-5
PAIR = 2
FLOPS = 2 * 2 * C * N


def write_identity(nc, pool, identity):
    ones = pool.tile([P, QUADRANT], F32, name="ones")
    nc.vector.memset(ones[:], 1.0)
    counts = pool.tile([P, QUADRANT], F32, name="counts", align_bytes=64)
    nc.vector.tensor_tensor_scan(counts[:], ones[:], ones[:], 0.0, ALU.mult, ALU.add)
    counts_turned = pool.tile([P, QUADRANT], F32, name="counts_turned", align_bytes=64)
    nc.vector.transpose(counts_turned[:], counts[:])
    nc.vector.memset(identity[:], 0.0)
    for q in range(0, P, QUADRANT):
        rows = slice(q, q + QUADRANT)
        nc.vector.tensor_tensor(identity[rows, rows], counts[rows, :], counts_turned[rows, :], ALU.is_equal)


def tile_first_decoder_kernel(tc, emb, pos, offs, out):
    nc = tc.nc
    emb_blocks = emb.rearrange("(b p) v -> b p v", p=P)
    pos_blocks = pos.rearrange("(b p) t -> b p t", p=P)
    out_blocks = out.rearrange("(b p) j -> p b j", p=P)

    with (
        tc.tile_pool(name="held", bufs=1) as held,
        tc.tile_pool(name="looked_up", bufs=1) as looked_up,
        tc.tile_pool(name="flip", bufs=FLIPPED * TB) as flip,
        tc.tile_pool(name="work", bufs=K - FLIPPED) as work,
        tc.psum_pool(name="banks", bufs=4) as banks,
        tc.psum_pool(name="backs", bufs=TB) as backs,
    ):
        offsets = held.tile([P, N // 16], U16, name="offsets")
        tables, codes = [], []
        for b in range(CB):
            table = held.tile([P, V], F32, name=f"table{b}")
            nc.sync.dma_start(table[:], emb_blocks[b])
            if b == 0:
                nc.sync.dma_start(offsets[:], offs)
            tables.append(table)
            code = held.tile([P, T], F32, name=f"code{b}")
            queue = nc.scalar if b == 0 else nc.sync
            queue.dma_start(code[:], pos_blocks[b])
            codes.append(code)
        code_copies = {}
        for k in range(1, K):
            copy = held.tile([P, CB, T], F32, name=f"code_copy{k}")
            for first in range(0, CB, PAIR):
                pair = slice(first, first + PAIR)
                nc.sync.dma_start(copy[:, pair, :], pos.rearrange("(b p) t -> p b t", p=P)[:, pair, :])
            code_copies[k] = copy

        eps = held.tile([P, 1], F32, name="eps")
        nc.vector.memset(eps[:], EPS)
        warm = held.tile([P, 1], F32, name="warm")
        nc.scalar.activation(warm[:], eps[:], FUNC.Abs_reciprocal_sqrt)

        average = held.tile([P, P], F32, name="average")
        nc.vector.memset(average[:], 1.0 / C)
        average16 = held.tile([P, P], BF16, name="average16")
        nc.vector.memset(average16[:], 1.0 / C)
        identity = held.tile([P, P], F32, name="identity")
        write_identity(nc, held, identity)

        for k in range(FLIPPED):
            piece = offsets[:, k * (T // 16) : (k + 1) * (T // 16)]
            flipped = [banks.tile([P, C], F32, name="flipped", tag="bank") for t in range(TB)]
            for b in range(CB):
                h = looked_up.tile([P, T], F32, name=f"h{b}")
                nc.vector.tensor_tensor(h[:], tables[b][:].indirect(piece), codes[b][:], ALU.add)
                for t in range(TB):
                    nc.tensor.transpose(flipped[t][:, b * P : (b + 1) * P], h[:, t * P : (t + 1) * P], identity[:])
            minus_means = []
            for t in range(TB):
                unread = flip.tile([P, C], F32, name="unread")
                minus_mean = flip.tile([P, 1], F32, name="minus_mean")
                nc.scalar.activation(unread[:], flipped[t][:], FUNC.Copy, scale=-1.0 / C, accum_out=minus_mean[:])
                minus_means.append(minus_mean)
            scales, shifts = [], []
            for t in range(TB):
                unread = flip.tile([P, C], F32, name="unread")
                squared = flip.tile([P, 1], F32, name="squared")
                nc.scalar.activation(
                    unread[:], flipped[t][:], FUNC.Square, bias=minus_means[t][:], accum_out=squared[:]
                )
                scale = flip.tile([P, 1], F32, name="scale")
                nc.scalar.activation(scale[:], squared[:], FUNC.Abs_reciprocal_sqrt, bias=eps[:], scale=1.0 / C)
                shift = flip.tile([P, 1], F32, name="shift")
                nc.scalar.activation(shift[:], minus_means[t][:], FUNC.Copy, scale=scale[:])
                scales.append(scale)
                shifts.append(shift)
            for t in range(TB):
                rows = flip.tile([P, C], F32, name="rows", tag="rows")
                nc.scalar.activation(rows[:], flipped[t][:], FUNC.Identity, bias=shifts[t][:], scale=scales[t][:])
                back = backs.tile([P, CB, P], F32, name="back")
                for b in range(CB):
                    nc.tensor.transpose(back[:, b, :], rows[:, b * P : (b + 1) * P], identity[:])
                y = flip.tile([P, CB, P], F32, name="flipped_y")
                nc.scalar.copy(y[:], back[:])
                first = k * T + t * P
                nc.sync.dma_start(out_blocks[:, :, first : first + P], y[:])

        hs, means = {}, {}
        for k in range(FLIPPED, K):
            piece = offsets[:, k * (T // 16) : (k + 1) * (T // 16)]
            h = work.tile([P, CB, T], F32, name="h")
            mean = banks.tile([P, T], F32, name="sum", tag="bank")
            for b in range(CB):
                nc.vector.tensor_tensor(h[:, b, :], tables[b][:].indirect(piece), code_copies[k][:, b, :], ALU.add)
                nc.tensor.matmul(mean[:], average[:], h[:, b, :], start=(b == 0), stop=(b == CB - 1))
            hs[k], means[k] = h, mean

        centred, rstds = {}, {}
        for k in range(FLIPPED, K):
            d = work.tile([P, CB, T], F32, name="d")
            squares = flip.tile([P, CB, T], BF16, name="squares", tag="rows")
            var = banks.tile([P, T], F32, name="sum", tag="bank")
            for first in range(0, CB, PAIR):
                pair = slice(first, first + PAIR)
                nc.vector.tensor_tensor(
                    d[:, pair, :],
                    hs[k][:, pair, :],
                    means[k][:].unsqueeze(1).to_broadcast([P, PAIR, T]),
                    ALU.subtract,
                )
                nc.scalar.activation(squares[:, pair, :], d[:, pair, :], FUNC.Square)
                for b in range(first, first + PAIR):
                    nc.tensor.matmul(var[:], average16[:], squares[:, b, :], start=(b == 0), stop=(b == CB - 1))
            rstd = work.tile([P, T], F32, name="rstd")
            nc.scalar.activation(rstd[:], var[:], FUNC.Abs_reciprocal_sqrt, bias=eps[:])
            centred[k], rstds[k] = d, rstd

        for k in range(FLIPPED, K):
            step = PAIR if k < K - 1 else 1
            for first in range(0, CB, step):
                y = work.tile([P, step, T], F32, name=f"y{first}_{step}")
                nc.vector.tensor_tensor(
                    y[:],
                    centred[k][:, first : first + step, :],
                    rstds[k][:].unsqueeze(1).to_broadcast([P, step, T]),
                    ALU.mult,
                )
                nc.sync.dma_start(out_blocks[:, first : first + step, k * T : (k + 1) * T], y[:])
